import numpy as np
import ml_dtypes


def mxq(x, axis, fmt="e4m3"):
    dtype, down = {"e4m3": (ml_dtypes.float8_e4m3fn, 7), "e5m2": (ml_dtypes.float8_e5m2, 14)}[fmt]
    v = np.moveaxis(np.asarray(x, np.float32).astype(ml_dtypes.bfloat16).astype(np.float64), axis, -1)
    blocks = v.reshape(v.shape[:-1] + (-1, 32))
    amax = np.abs(blocks).max(-1, keepdims=True)
    byte = np.maximum(np.where(amax > 0, np.frexp(amax)[1] - 1 + 127, 0) - down, 1)
    scale = np.exp2(byte - 127.0)
    codes = (blocks / scale).astype(np.float32).astype(dtype).astype(np.float64)
    return np.moveaxis((codes * scale).reshape(v.shape), -1, axis)


WIDE = False


def mx_kscale(k):
    if not WIDE:
        return np.ones(k)
    levels = np.array([10, -10, 5, -5, 0])
    a = np.random.permutation(np.resize(levels, k // 512 * 4)).reshape(k // 512, 4)
    idx = np.arange(k)
    return np.exp2(a[idx // 512, idx % 128 // 32])


BF16 = ml_dtypes.bfloat16


def bf(x):
    return np.asarray(x, np.float32).astype(BF16)


def f64(x):
    return np.asarray(x).astype(np.float64)


B, D_IN, D_FEAT, N_EX, N_LAB = 128, 512, 1024, 1024, 128
P_FACTOR = 3.0
EPS = 1e-12


def unit_rows(x):
    return x / np.sqrt((x * x).sum(-1, keepdims=True))


def l1_normalize(x):
    n = np.abs(x).sum(-1, keepdims=True)
    return x / np.maximum(n, EPS)


def setup_inputs():
    s = mx_kscale(D_FEAT)
    return {"f_norm": bf(unit_rows(np.random.standard_normal((B, D_FEAT))) * s),
            "e_norm": bf(unit_rows(np.random.standard_normal((N_EX, D_FEAT))) / s),
            "ex_class_reps": bf(np.random.standard_normal((N_EX, N_LAB)) * 0.0625 * np.sqrt(N_EX))}


def reference(f_norm, e_norm, ex_class_reps):
    s = mxq(f64(f_norm), 1, "e4m3") @ mxq(f64(e_norm), 1, "e4m3").T
    a = np.sign(s) * np.abs(s) ** P_FACTOR
    a = l1_normalize(a)
    return mxq(a, 1, "e4m3") @ mxq(f64(ex_class_reps), 0, "e4m3")

@@ -1,0 +1,191 @@
+from contextlib import ExitStack
+
+import concourse.mybir as mybir
+from concourse.masks import make_identity
+
+F32 = mybir.dt.float32
+BF16 = mybir.dt.bfloat16
+U32 = mybir.dt.uint32
+U8 = mybir.dt.uint8
+FP8X4 = mybir.dt.float8_e4m3fn_x4
+ALU = mybir.AluOpType
+ACT = mybir.ActivationFunctionType
+
+P = 128
+PACK = 4
+K_PASS = P * PACK
+
+N_QUERY = 128
+N_FEAT = 1024
+N_EX = 1024
+N_LABEL = 128
+EPS = 1e-12
+
+FEAT_PASSES = N_FEAT // K_PASS
+EX_PASSES = N_EX // K_PASS
+EX_TILES = N_EX // P
+WORD_BLOCKS = N_FEAT // 2 // P
+CHUNK_TILES = 2
+N_CHUNKS = EX_TILES // CHUNK_TILES
+
+FLOPS = 2 * N_QUERY * N_FEAT * N_EX + 2 * N_QUERY * N_EX * N_LABEL
+
+
+def transpose_rows(nc, psum_xt, rows, identity):
+    words = rows.bitcast(F32)
+    xt = psum_xt.tile([P, WORD_BLOCKS, P], F32)
+    for w in range(WORD_BLOCKS):
+        nc.tensor.transpose(xt[:, w, :], words[:, w * P : (w + 1) * P], identity[:])
+    return xt
+
+
+def group_features(copy, xt, grouped):
+    copy(
+        out=grouped.bitcast(F32).rearrange("p (c r u) -> p c r u", c=FEAT_PASSES, u=2),
+        in_=xt[:].rearrange("p (c u) r -> p c r u", u=2),
+    )
+
+
+def tile_minerva_pa_s_kernel(tc, f_norm, e_norm, ex_class_reps, out):
+    nc = tc.nc
+    with ExitStack() as stack:
+        keep = stack.enter_context(tc.tile_pool(name="keep", bufs=1))
+        chunks = stack.enter_context(tc.tile_pool(name="chunks", bufs=N_CHUNKS))
+        psum_xt = stack.enter_context(tc.psum_pool(name="psum_xt", bufs=4))
+        psum_s = stack.enter_context(tc.psum_pool(name="psum_s", bufs=2))
+        psum_norm = stack.enter_context(tc.psum_pool(name="psum_norm", bufs=1))
+
+        e_view = e_norm.rearrange("(g p t) d -> p g t d", p=P, t=PACK)
+        r_view = ex_class_reps.rearrange("(g p t) n -> p g t n", p=P, t=PACK)
+
+        f_rows = keep.tile([P, N_FEAT], BF16)
+        nc.sync.dma_start(out=f_rows[:], in_=f_norm)
+        r_rows = keep.tile([P, EX_PASSES, PACK, N_LABEL], BF16)
+        e_rows = []
+        for j in range(N_CHUNKS):
+            first = j * CHUNK_TILES
+            g, t = first // PACK, first % PACK
+            e_chunk = chunks.tile([P, CHUNK_TILES, N_FEAT], BF16, name="e_chunk")
+            nc.sync.dma_start(out=e_chunk[:], in_=e_view[:, g, t : t + CHUNK_TILES, :])
+            e_rows.append(e_chunk)
+            if j == 0:
+                nc.sync.dma_start(out=r_rows[:], in_=r_view)
+
+        identity = keep.tile([P, P], F32)
+        make_identity(nc, identity[:])
+        ones = keep.tile([P, 2], F32)
+        nc.vector.memset(ones[:], 1.0)
+        table_warm = keep.tile([P, 2], F32)
+        nc.scalar.activation(out=table_warm[:], in_=ones[:], func=ACT.Square)
+
+        f_grouped = keep.tile([P, N_FEAT], BF16, align_bytes=64)
+        f_codes = keep.tile([P, FEAT_PASSES, N_QUERY], U32, align_bytes=64)
+        f_scales = keep.tile([P, FEAT_PASSES, N_QUERY], U8, align_bytes=64)
+        f_xt = transpose_rows(nc, psum_xt, f_rows[:], identity)
+        group_features(nc.scalar.copy, f_xt, f_grouped[:])
+        nc.vector.quantize_mx(
+            out=f_codes[:].rearrange("p c q -> p (c q)").bitcast(FP8X4),
+            scales=f_scales[:].rearrange("p c q -> p (c q)"),
+            in_=f_grouped[:],
+        )
+
+        r_grouped = keep.tile([P, EX_PASSES, N_LABEL, PACK], BF16, align_bytes=64)
+        r_codes = keep.tile([P, EX_PASSES, N_LABEL], U32, align_bytes=64)
+        r_scales = keep.tile([P, EX_PASSES, N_LABEL], U8, align_bytes=64)
+        nc.vector.tensor_copy(out=r_grouped[:], in_=r_rows[:].rearrange("p g t n -> p g n t"))
+        nc.vector.quantize_mx(
+            out=r_codes[:].rearrange("p g n -> p (g n)").bitcast(FP8X4),
+            scales=r_scales[:].rearrange("p g n -> p (g n)"),
+            in_=r_grouped[:].rearrange("p g n t -> p (g n t)"),
+        )
+
+        cubes = keep.tile([P, EX_TILES, N_QUERY], F32)
+        rowsum_ps = psum_norm.tile([P, 2], F32)
+        for j in range(N_CHUNKS):
+            e_grouped = chunks.tile([P, CHUNK_TILES, N_FEAT], BF16, align_bytes=64)
+            for i in range(CHUNK_TILES):
+                e_xt = transpose_rows(nc, psum_xt, e_rows[j][:, i, :], identity)
+                copy = nc.scalar.copy if i % 2 == 0 else nc.vector.tensor_copy
+                group_features(copy, e_xt, e_grouped[:, i, :])
+
+            e_codes = chunks.tile([P, CHUNK_TILES, FEAT_PASSES, P], U32, align_bytes=64)
+            e_scales = chunks.tile([P, CHUNK_TILES, FEAT_PASSES, P], U8, align_bytes=64)
+            nc.vector.quantize_mx(
+                out=e_codes[:].rearrange("p i c x -> p (i c x)").bitcast(FP8X4),
+                scales=e_scales[:].rearrange("p i c x -> p (i c x)"),
+                in_=e_grouped[:].rearrange("p i k -> p (i k)"),
+            )
+
+            s_ps = psum_s.tile([P, CHUNK_TILES, N_QUERY], F32)
+            for i in range(CHUNK_TILES):
+                for c in range(FEAT_PASSES):
+                    nc.tensor.matmul_mx(
+                        out=s_ps[:, i, :],
+                        lhsT=e_codes[:, i, c, :].bitcast(FP8X4),
+                        lhsT_scale=e_scales[:, i, c, :],
+                        rhs=f_codes[:, c, :].bitcast(FP8X4),
+                        rhs_scale=f_scales[:, c, :],
+                        start=(c == 0),
+                        stop=(c == FEAT_PASSES - 1),
+                    )
+
+            chunk_cubes = cubes[:, j * CHUNK_TILES : (j + 1) * CHUNK_TILES, :]
+            squares = chunks.tile([P, CHUNK_TILES, N_QUERY], F32)
+            nc.scalar.activation(out=squares[:], in_=s_ps[:], func=ACT.Square)
+            nc.vector.tensor_tensor(out=chunk_cubes, in0=s_ps[:], in1=squares[:], op=ALU.mult)
+
+            abs_cubes = chunks.tile([P, CHUNK_TILES, N_QUERY], F32)
+            nc.scalar.activation(out=abs_cubes[:], in_=chunk_cubes, func=ACT.Abs)
+            for i in range(CHUNK_TILES):
+                tile_index = j * CHUNK_TILES + i
+                nc.tensor.matmul(
+                    rowsum_ps[:],
+                    lhsT=abs_cubes[:, i, :],
+                    rhs=ones[:],
+                    start=(tile_index == 0),
+                    stop=(tile_index == EX_TILES - 1),
+                )
+
+        rowsum = keep.tile([P, 1], F32)
+        nc.vector.tensor_scalar_max(out=rowsum[:], in0=rowsum_ps[:, 0:1], scalar1=EPS)
+        inverse = keep.tile([P, 1], F32)
+        nc.vector.reciprocal(out=inverse[:], in_=rowsum[:])
+        inverse_ps = psum_norm.tile([P, N_QUERY], F32)
+        nc.tensor.matmul(
+            inverse_ps[:],
+            lhsT=inverse[:, 0:1].to_broadcast([P, P]),
+            rhs=identity[:],
+            start=True,
+            stop=True,
+        )
+
+        p_grouped = keep.tile([P, EX_PASSES, N_QUERY, PACK], BF16, align_bytes=64)
+        p_codes = keep.tile([P, EX_PASSES, N_QUERY], U32, align_bytes=64)
+        p_scales = keep.tile([P, EX_PASSES, N_QUERY], U8, align_bytes=64)
+        for g in range(EX_PASSES):
+            nc.vector.tensor_tensor(
+                out=p_grouped[:, g, :, :],
+                in0=cubes[:, g * PACK : (g + 1) * PACK, :].rearrange("p t q -> p q t"),
+                in1=inverse_ps[:].unsqueeze(2).to_broadcast([P, N_QUERY, PACK]),
+                op=ALU.mult,
+            )
+        nc.vector.quantize_mx(
+            out=p_codes[:].rearrange("p g q -> p (g q)").bitcast(FP8X4),
+            scales=p_scales[:].rearrange("p g q -> p (g q)"),
+            in_=p_grouped[:].rearrange("p g q t -> p (g q t)"),
+        )
+
+        echo_ps = psum_s.tile([P, N_LABEL], F32, tag="s_ps")
+        for g in range(EX_PASSES):
+            nc.tensor.matmul_mx(
+                out=echo_ps[:],
+                lhsT=p_codes[:, g, :].bitcast(FP8X4),
+                lhsT_scale=p_scales[:, g, :],
+                rhs=r_codes[:, g, :].bitcast(FP8X4),
+                rhs_scale=r_scales[:, g, :],
+                start=(g == 0),
+                stop=(g == EX_PASSES - 1),
+            )
+        echo = keep.tile([P, N_LABEL], F32)
+        nc.vector.tensor_copy(out=echo[:], in_=echo_ps[:])
+        nc.sync.dma_start(out=out, in_=echo[:])

@@ -49,9 +49,10 @@ def group_features(copy, xt, grouped):
 def tile_minerva_pa_s_kernel(tc, f_norm, e_norm, ex_class_reps, out):
     nc = tc.nc
     with ExitStack() as stack:
+        stack.enter_context(tc.manual_schedule())
         keep = stack.enter_context(tc.tile_pool(name="keep", bufs=1))
         chunks = stack.enter_context(tc.tile_pool(name="chunks", bufs=N_CHUNKS))
-        psum_xt = stack.enter_context(tc.psum_pool(name="psum_xt", bufs=4))
+        psum_xt = stack.enter_context(tc.psum_pool(name="psum_xt", bufs=2 * CHUNK_TILES))
         psum_s = stack.enter_context(tc.psum_pool(name="psum_s", bufs=2))
         psum_norm = stack.enter_context(tc.psum_pool(name="psum_norm", bufs=1))
 
@@ -60,7 +61,6 @@ def tile_minerva_pa_s_kernel(tc, f_norm, e_norm, ex_class_reps, out):
 
         f_rows = keep.tile([P, N_FEAT], BF16)
         nc.sync.dma_start(out=f_rows[:], in_=f_norm)
-        r_rows = keep.tile([P, EX_PASSES, PACK, N_LABEL], BF16)
         e_rows = []
         for j in range(N_CHUNKS):
             first = j * CHUNK_TILES
@@ -68,15 +68,15 @@ def tile_minerva_pa_s_kernel(tc, f_norm, e_norm, ex_class_reps, out):
             e_chunk = chunks.tile([P, CHUNK_TILES, N_FEAT], BF16, name="e_chunk")
             nc.sync.dma_start(out=e_chunk[:], in_=e_view[:, g, t : t + CHUNK_TILES, :])
             e_rows.append(e_chunk)
-            if j == 0:
-                nc.sync.dma_start(out=r_rows[:], in_=r_view)
+        r_rows = keep.tile([P, EX_PASSES, PACK, N_LABEL], BF16)
+        nc.sync.dma_start(out=r_rows[:], in_=r_view)
 
         identity = keep.tile([P, P], F32)
         make_identity(nc, identity[:])
         ones = keep.tile([P, 2], F32)
         nc.vector.memset(ones[:], 1.0)
         table_warm = keep.tile([P, 2], F32)
-        nc.scalar.activation(out=table_warm[:], in_=ones[:], func=ACT.Square)
+        nc.scalar.activation(out=table_warm[:], in_=ones[:], func=ACT.Abs)
 
         f_grouped = keep.tile([P, N_FEAT], BF16, align_bytes=64)
         f_codes = keep.tile([P, FEAT_PASSES, N_QUERY], U32, align_bytes=64)
@@ -89,53 +89,51 @@ def tile_minerva_pa_s_kernel(tc, f_norm, e_norm, ex_class_reps, out):
             in_=f_grouped[:],
         )
 
-        r_grouped = keep.tile([P, EX_PASSES, N_LABEL, PACK], BF16, align_bytes=64)
-        r_codes = keep.tile([P, EX_PASSES, N_LABEL], U32, align_bytes=64)
-        r_scales = keep.tile([P, EX_PASSES, N_LABEL], U8, align_bytes=64)
-        nc.vector.tensor_copy(out=r_grouped[:], in_=r_rows[:].rearrange("p g t n -> p g n t"))
-        nc.vector.quantize_mx(
-            out=r_codes[:].rearrange("p g n -> p (g n)").bitcast(FP8X4),
-            scales=r_scales[:].rearrange("p g n -> p (g n)"),
-            in_=r_grouped[:].rearrange("p g n t -> p (g n t)"),
-        )
-
         cubes = keep.tile([P, EX_TILES, N_QUERY], F32)
         rowsum_ps = psum_norm.tile([P, 2], F32)
-        for j in range(N_CHUNKS):
-            e_grouped = chunks.tile([P, CHUNK_TILES, N_FEAT], BF16, align_bytes=64)
+        e_grouped, e_codes, e_scales, s_ps, squares = {}, {}, {}, {}, {}
+
+        def transpose_chunk(j):
+            e_grouped[j] = chunks.tile([P, CHUNK_TILES, N_FEAT], BF16, name="e_grouped", align_bytes=64)
             for i in range(CHUNK_TILES):
                 e_xt = transpose_rows(nc, psum_xt, e_rows[j][:, i, :], identity)
                 copy = nc.scalar.copy if i % 2 == 0 else nc.vector.tensor_copy
-                group_features(copy, e_xt, e_grouped[:, i, :])
+                group_features(copy, e_xt, e_grouped[j][:, i, :])
 
-            e_codes = chunks.tile([P, CHUNK_TILES, FEAT_PASSES, P], U32, align_bytes=64)
-            e_scales = chunks.tile([P, CHUNK_TILES, FEAT_PASSES, P], U8, align_bytes=64)
+        def quantise_chunk(j):
+            e_codes[j] = chunks.tile([P, CHUNK_TILES, FEAT_PASSES, P], U32, name="e_codes", align_bytes=64)
+            e_scales[j] = chunks.tile([P, CHUNK_TILES, FEAT_PASSES, P], U8, name="e_scales", align_bytes=64)
             nc.vector.quantize_mx(
-                out=e_codes[:].rearrange("p i c x -> p (i c x)").bitcast(FP8X4),
-                scales=e_scales[:].rearrange("p i c x -> p (i c x)"),
-                in_=e_grouped[:].rearrange("p i k -> p (i k)"),
+                out=e_codes[j][:].rearrange("p i c x -> p (i c x)").bitcast(FP8X4),
+                scales=e_scales[j][:].rearrange("p i c x -> p (i c x)"),
+                in_=e_grouped[j][:].rearrange("p i k -> p (i k)"),
             )
 
-            s_ps = psum_s.tile([P, CHUNK_TILES, N_QUERY], F32)
+        def score_chunk(j):
+            s_ps[j] = psum_s.tile([P, CHUNK_TILES, N_QUERY], F32, name="s_ps")
             for i in range(CHUNK_TILES):
                 for c in range(FEAT_PASSES):
                     nc.tensor.matmul_mx(
-                        out=s_ps[:, i, :],
-                        lhsT=e_codes[:, i, c, :].bitcast(FP8X4),
-                        lhsT_scale=e_scales[:, i, c, :],
+                        out=s_ps[j][:, i, :],
+                        lhsT=e_codes[j][:, i, c, :].bitcast(FP8X4),
+                        lhsT_scale=e_scales[j][:, i, c, :],
                         rhs=f_codes[:, c, :].bitcast(FP8X4),
                         rhs_scale=f_scales[:, c, :],
                         start=(c == 0),
                         stop=(c == FEAT_PASSES - 1),
                     )
+            squares[j] = chunks.tile([P, CHUNK_TILES, N_QUERY], F32, name="squares")
+            nc.scalar.activation(out=squares[j][:], in_=s_ps[j][:], func=ACT.Square)
 
-            chunk_cubes = cubes[:, j * CHUNK_TILES : (j + 1) * CHUNK_TILES, :]
-            squares = chunks.tile([P, CHUNK_TILES, N_QUERY], F32)
-            nc.scalar.activation(out=squares[:], in_=s_ps[:], func=ACT.Square)
-            nc.vector.tensor_tensor(out=chunk_cubes, in0=s_ps[:], in1=squares[:], op=ALU.mult)
+        def chunk_cubes(j):
+            return cubes[:, j * CHUNK_TILES : (j + 1) * CHUNK_TILES, :]
 
+        def cube_chunk(j):
+            nc.vector.tensor_tensor(out=chunk_cubes(j), in0=s_ps[j][:], in1=squares[j][:], op=ALU.mult)
+
+        def sum_chunk(j):
             abs_cubes = chunks.tile([P, CHUNK_TILES, N_QUERY], F32)
-            nc.scalar.activation(out=abs_cubes[:], in_=chunk_cubes, func=ACT.Abs)
+            nc.scalar.activation(out=abs_cubes[:], in_=chunk_cubes(j), func=ACT.Abs)
             for i in range(CHUNK_TILES):
                 tile_index = j * CHUNK_TILES + i
                 nc.tensor.matmul(
@@ -145,6 +143,23 @@ def tile_minerva_pa_s_kernel(tc, f_norm, e_norm, ex_class_reps, out):
                     start=(tile_index == 0),
                     stop=(tile_index == EX_TILES - 1),
                 )
+
+        for k in range(N_CHUNKS + 2):
+            if k < N_CHUNKS:
+                transpose_chunk(k)
+            if k >= 2:
+                cube_chunk(k - 2)
+            if k < N_CHUNKS:
+                quantise_chunk(k)
+            if 1 <= k <= N_CHUNKS:
+                score_chunk(k - 1)
+            if k >= 2:
+                sum_chunk(k - 2)
+
+        r_grouped = keep.tile([P, EX_PASSES, N_LABEL, PACK], BF16, align_bytes=64)
+        r_codes = keep.tile([P, EX_PASSES, N_LABEL], U32, align_bytes=64)
+        r_scales = keep.tile([P, EX_PASSES, N_LABEL], U8, align_bytes=64)
+        nc.vector.tensor_copy(out=r_grouped[:], in_=r_rows[:].rearrange("p g t n -> p g n t"))
 
         rowsum = keep.tile([P, 1], F32)
         nc.vector.tensor_scalar_max(out=rowsum[:], in0=rowsum_ps[:, 0:1], scalar1=EPS)
@@ -158,6 +173,11 @@ def tile_minerva_pa_s_kernel(tc, f_norm, e_norm, ex_class_reps, out):
             start=True,
             stop=True,
         )
+        nc.vector.quantize_mx(
+            out=r_codes[:].rearrange("p g n -> p (g n)").bitcast(FP8X4),
+            scales=r_scales[:].rearrange("p g n -> p (g n)"),
+            in_=r_grouped[:].rearrange("p g n t -> p (g n t)"),
+        )
 
         p_grouped = keep.tile([P, EX_PASSES, N_QUERY, PACK], BF16, align_bytes=64)
         p_codes = keep.tile([P, EX_PASSES, N_QUERY], U32, align_bytes=64)
@@ -169,11 +189,12 @@ def tile_minerva_pa_s_kernel(tc, f_norm, e_norm, ex_class_reps, out):
                 in1=inverse_ps[:].unsqueeze(2).to_broadcast([P, N_QUERY, PACK]),
                 op=ALU.mult,
             )
-        nc.vector.quantize_mx(
-            out=p_codes[:].rearrange("p g q -> p (g q)").bitcast(FP8X4),
-            scales=p_scales[:].rearrange("p g q -> p (g q)"),
-            in_=p_grouped[:].rearrange("p g q t -> p (g q t)"),
-        )
+        for g in range(EX_PASSES):
+            nc.vector.quantize_mx(
+                out=p_codes[:, g, :].bitcast(FP8X4),
+                scales=p_scales[:, g, :],
+                in_=p_grouped[:, g, :, :].rearrange("p q t -> p (q t)"),
+            )
 
         echo_ps = psum_s.tile([P, N_LABEL], F32, tag="s_ps")
         for g in range(EX_PASSES):
@@ -187,5 +208,5 @@ def tile_minerva_pa_s_kernel(tc, f_norm, e_norm, ex_class_reps, out):
                 stop=(g == EX_PASSES - 1),
             )
         echo = keep.tile([P, N_LABEL], F32)
-        nc.vector.tensor_copy(out=echo[:], in_=echo_ps[:])
+        nc.scalar.copy(out=echo[:], in_=echo_ps[:])
         nc.sync.dma_start(out=out, in_=echo[:])

@@ -28,6 +28,10 @@ WORD_BLOCKS = N_FEAT // 2 // P
 CHUNK_TILES = 2
 N_CHUNKS = EX_TILES // CHUNK_TILES
 
+SCORE_LAG = 2
+CUBE_LAG = 3
+SUM_LAG = 5
+
 FLOPS = 2 * N_QUERY * N_FEAT * N_EX + 2 * N_QUERY * N_EX * N_LABEL
 
 
@@ -51,6 +55,7 @@ def tile_minerva_pa_s_kernel(tc, f_norm, e_norm, ex_class_reps, out):
     with ExitStack() as stack:
         stack.enter_context(tc.manual_schedule())
         keep = stack.enter_context(tc.tile_pool(name="keep", bufs=1))
+        tiles = stack.enter_context(tc.tile_pool(name="tiles", bufs=EX_TILES))
         chunks = stack.enter_context(tc.tile_pool(name="chunks", bufs=N_CHUNKS))
         psum_xt = stack.enter_context(tc.psum_pool(name="psum_xt", bufs=2 * CHUNK_TILES))
         psum_s = stack.enter_context(tc.psum_pool(name="psum_s", bufs=2))
@@ -62,12 +67,11 @@ def tile_minerva_pa_s_kernel(tc, f_norm, e_norm, ex_class_reps, out):
         f_rows = keep.tile([P, N_FEAT], BF16)
         nc.sync.dma_start(out=f_rows[:], in_=f_norm)
         e_rows = []
-        for j in range(N_CHUNKS):
-            first = j * CHUNK_TILES
-            g, t = first // PACK, first % PACK
-            e_chunk = chunks.tile([P, CHUNK_TILES, N_FEAT], BF16, name="e_chunk")
-            nc.sync.dma_start(out=e_chunk[:], in_=e_view[:, g, t : t + CHUNK_TILES, :])
-            e_rows.append(e_chunk)
+        for g in range(EX_PASSES):
+            for t in range(PACK):
+                e_tile = tiles.tile([P, N_FEAT], BF16, name="e_tile")
+                nc.sync.dma_start(out=e_tile[:], in_=e_view[:, g, t, :])
+                e_rows.append(e_tile)
         r_rows = keep.tile([P, EX_PASSES, PACK, N_LABEL], BF16)
         nc.sync.dma_start(out=r_rows[:], in_=r_view)
 
@@ -91,14 +95,13 @@ def tile_minerva_pa_s_kernel(tc, f_norm, e_norm, ex_class_reps, out):
 
         cubes = keep.tile([P, EX_TILES, N_QUERY], F32)
         rowsum_ps = psum_norm.tile([P, 2], F32)
-        e_grouped, e_codes, e_scales, s_ps, squares = {}, {}, {}, {}, {}
+        e_grouped, e_codes, e_scales, s_ps, squares, abs_cubes = {}, {}, {}, {}, {}, {}
 
         def transpose_chunk(j):
             e_grouped[j] = chunks.tile([P, CHUNK_TILES, N_FEAT], BF16, name="e_grouped", align_bytes=64)
             for i in range(CHUNK_TILES):
-                e_xt = transpose_rows(nc, psum_xt, e_rows[j][:, i, :], identity)
-                copy = nc.scalar.copy if i % 2 == 0 else nc.vector.tensor_copy
-                group_features(copy, e_xt, e_grouped[j][:, i, :])
+                e_xt = transpose_rows(nc, psum_xt, e_rows[j * CHUNK_TILES + i][:], identity)
+                group_features(nc.scalar.copy, e_xt, e_grouped[j][:, i, :])
 
         def quantise_chunk(j):
             e_codes[j] = chunks.tile([P, CHUNK_TILES, FEAT_PASSES, P], U32, name="e_codes", align_bytes=64)
@@ -131,48 +134,44 @@ def tile_minerva_pa_s_kernel(tc, f_norm, e_norm, ex_class_reps, out):
         def cube_chunk(j):
             nc.vector.tensor_tensor(out=chunk_cubes(j), in0=s_ps[j][:], in1=squares[j][:], op=ALU.mult)
 
+        def abs_chunk(j):
+            abs_cubes[j] = chunks.tile([P, CHUNK_TILES, N_QUERY], F32, name="abs_cubes")
+            nc.scalar.activation(out=abs_cubes[j][:], in_=chunk_cubes(j), func=ACT.Abs)
+
         def sum_chunk(j):
-            abs_cubes = chunks.tile([P, CHUNK_TILES, N_QUERY], F32)
-            nc.scalar.activation(out=abs_cubes[:], in_=chunk_cubes(j), func=ACT.Abs)
             for i in range(CHUNK_TILES):
                 tile_index = j * CHUNK_TILES + i
                 nc.tensor.matmul(
                     rowsum_ps[:],
-                    lhsT=abs_cubes[:, i, :],
+                    lhsT=abs_cubes[j][:, i, :],
                     rhs=ones[:],
                     start=(tile_index == 0),
                     stop=(tile_index == EX_TILES - 1),
                 )
 
-        for k in range(N_CHUNKS + 2):
+        for k in range(N_CHUNKS + SUM_LAG):
             if k < N_CHUNKS:
                 transpose_chunk(k)
-            if k >= 2:
-                cube_chunk(k - 2)
+            if 0 <= k - CUBE_LAG < N_CHUNKS:
+                cube_chunk(k - CUBE_LAG)
             if k < N_CHUNKS:
                 quantise_chunk(k)
-            if 1 <= k <= N_CHUNKS:
-                score_chunk(k - 1)
-            if k >= 2:
-                sum_chunk(k - 2)
+            if 0 <= k - SCORE_LAG < N_CHUNKS:
+                score_chunk(k - SCORE_LAG)
+            if 0 <= k - CUBE_LAG < N_CHUNKS:
+                abs_chunk(k - CUBE_LAG)
+            if 0 <= k - SUM_LAG:
+                sum_chunk(k - SUM_LAG)
 
         r_grouped = keep.tile([P, EX_PASSES, N_LABEL, PACK], BF16, align_bytes=64)
         r_codes = keep.tile([P, EX_PASSES, N_LABEL], U32, align_bytes=64)
         r_scales = keep.tile([P, EX_PASSES, N_LABEL], U8, align_bytes=64)
         nc.vector.tensor_copy(out=r_grouped[:], in_=r_rows[:].rearrange("p g t n -> p g n t"))
 
-        rowsum = keep.tile([P, 1], F32)
-        nc.vector.tensor_scalar_max(out=rowsum[:], in0=rowsum_ps[:, 0:1], scalar1=EPS)
         inverse = keep.tile([P, 1], F32)
-        nc.vector.reciprocal(out=inverse[:], in_=rowsum[:])
+        nc.vector.reciprocal(out=inverse[:], in_=rowsum_ps[:, 0:1])
         inverse_ps = psum_norm.tile([P, N_QUERY], F32)
-        nc.tensor.matmul(
-            inverse_ps[:],
-            lhsT=inverse[:, 0:1].to_broadcast([P, P]),
-            rhs=identity[:],
-            start=True,
-            stop=True,
-        )
+        nc.tensor.transpose(inverse_ps[:], inverse[:, 0:1].to_broadcast([P, P]), identity[:])
         nc.vector.quantize_mx(
             out=r_codes[:].rearrange("p g n -> p (g n)").bitcast(FP8X4),
             scales=r_scales[:].rearrange("p g n -> p (g n)"),
@@ -183,11 +182,13 @@ def tile_minerva_pa_s_kernel(tc, f_norm, e_norm, ex_class_reps, out):
         p_codes = keep.tile([P, EX_PASSES, N_QUERY], U32, align_bytes=64)
         p_scales = keep.tile([P, EX_PASSES, N_QUERY], U8, align_bytes=64)
         for g in range(EX_PASSES):
-            nc.vector.tensor_tensor(
+            nc.vector.scalar_tensor_tensor(
                 out=p_grouped[:, g, :, :],
-                in0=cubes[:, g * PACK : (g + 1) * PACK, :].rearrange("p t q -> p q t"),
-                in1=inverse_ps[:].unsqueeze(2).to_broadcast([P, N_QUERY, PACK]),
-                op=ALU.mult,
+                in0=inverse_ps[:].unsqueeze(2).to_broadcast([P, N_QUERY, PACK]),
+                scalar=1.0 / EPS,
+                in1=cubes[:, g * PACK : (g + 1) * PACK, :].rearrange("p t q -> p q t"),
+                op0=ALU.min,
+                op1=ALU.mult,
             )
         for g in range(EX_PASSES):
             nc.vector.quantize_mx(

@@ -25,12 +25,9 @@ FEAT_PASSES = N_FEAT // K_PASS
 EX_PASSES = N_EX // K_PASS
 EX_TILES = N_EX // P
 WORD_BLOCKS = N_FEAT // 2 // P
-CHUNK_TILES = 2
-N_CHUNKS = EX_TILES // CHUNK_TILES
-
-SCORE_LAG = 2
-CUBE_LAG = 3
-SUM_LAG = 5
+UNIT_TILES = 2
+N_UNITS = EX_TILES // UNIT_TILES
+SUM_COLS = 64
 
 FLOPS = 2 * N_QUERY * N_FEAT * N_EX + 2 * N_QUERY * N_EX * N_LABEL
 
@@ -56,10 +53,10 @@ def tile_minerva_pa_s_kernel(tc, f_norm, e_norm, ex_class_reps, out):
         stack.enter_context(tc.manual_schedule())
         keep = stack.enter_context(tc.tile_pool(name="keep", bufs=1))
         tiles = stack.enter_context(tc.tile_pool(name="tiles", bufs=EX_TILES))
-        chunks = stack.enter_context(tc.tile_pool(name="chunks", bufs=N_CHUNKS))
-        psum_xt = stack.enter_context(tc.psum_pool(name="psum_xt", bufs=2 * CHUNK_TILES))
-        psum_s = stack.enter_context(tc.psum_pool(name="psum_s", bufs=2))
-        psum_norm = stack.enter_context(tc.psum_pool(name="psum_norm", bufs=1))
+        units = stack.enter_context(tc.tile_pool(name="units", bufs=N_UNITS))
+        psum_xt = stack.enter_context(tc.psum_pool(name="psum_xt", bufs=3))
+        psum_s = stack.enter_context(tc.psum_pool(name="psum_s", bufs=N_UNITS))
+        psum_sum = stack.enter_context(tc.psum_pool(name="psum_sum", bufs=1))
 
         e_view = e_norm.rearrange("(g p t) d -> p g t d", p=P, t=PACK)
         r_view = ex_class_reps.rearrange("(g p t) n -> p g t n", p=P, t=PACK)
@@ -77,10 +74,10 @@ def tile_minerva_pa_s_kernel(tc, f_norm, e_norm, ex_class_reps, out):
 
         identity = keep.tile([P, P], F32)
         make_identity(nc, identity[:])
-        ones = keep.tile([P, 2], F32)
+        ones = keep.tile([P, SUM_COLS], F32)
         nc.vector.memset(ones[:], 1.0)
-        table_warm = keep.tile([P, 2], F32)
-        nc.scalar.activation(out=table_warm[:], in_=ones[:], func=ACT.Abs)
+        table_warm = keep.tile([P, 1], F32)
+        nc.scalar.activation(out=table_warm[:], in_=ones[:, 0:1], func=ACT.Abs)
 
         f_grouped = keep.tile([P, N_FEAT], BF16, align_bytes=64)
         f_codes = keep.tile([P, FEAT_PASSES, N_QUERY], U32, align_bytes=64)
@@ -94,74 +91,73 @@ def tile_minerva_pa_s_kernel(tc, f_norm, e_norm, ex_class_reps, out):
         )
 
         cubes = keep.tile([P, EX_TILES, N_QUERY], F32)
-        rowsum_ps = psum_norm.tile([P, 2], F32)
+        rowsum_ps = psum_sum.tile([P, SUM_COLS], F32)
         e_grouped, e_codes, e_scales, s_ps, squares, abs_cubes = {}, {}, {}, {}, {}, {}
 
-        def transpose_chunk(j):
-            e_grouped[j] = chunks.tile([P, CHUNK_TILES, N_FEAT], BF16, name="e_grouped", align_bytes=64)
-            for i in range(CHUNK_TILES):
-                e_xt = transpose_rows(nc, psum_xt, e_rows[j * CHUNK_TILES + i][:], identity)
-                group_features(nc.scalar.copy, e_xt, e_grouped[j][:, i, :])
+        def transpose_tile(i):
+            e_xt = transpose_rows(nc, psum_xt, e_rows[i][:], identity)
+            e_grouped[i] = tiles.tile([P, N_FEAT], BF16, name="e_grouped", align_bytes=64)
+            copy = nc.vector.tensor_copy if i % 3 == 2 else nc.scalar.copy
+            group_features(copy, e_xt, e_grouped[i][:])
 
-        def quantise_chunk(j):
-            e_codes[j] = chunks.tile([P, CHUNK_TILES, FEAT_PASSES, P], U32, name="e_codes", align_bytes=64)
-            e_scales[j] = chunks.tile([P, CHUNK_TILES, FEAT_PASSES, P], U8, name="e_scales", align_bytes=64)
+        def quantise_tile(i):
+            e_codes[i] = tiles.tile([P, FEAT_PASSES, P], U32, name="e_codes", align_bytes=64)
+            e_scales[i] = tiles.tile([P, FEAT_PASSES, P], U8, name="e_scales", align_bytes=64)
             nc.vector.quantize_mx(
-                out=e_codes[j][:].rearrange("p i c x -> p (i c x)").bitcast(FP8X4),
-                scales=e_scales[j][:].rearrange("p i c x -> p (i c x)"),
-                in_=e_grouped[j][:].rearrange("p i k -> p (i k)"),
+                out=e_codes[i][:].rearrange("p c x -> p (c x)").bitcast(FP8X4),
+                scales=e_scales[i][:].rearrange("p c x -> p (c x)"),
+                in_=e_grouped[i][:],
             )
 
-        def score_chunk(j):
-            s_ps[j] = psum_s.tile([P, CHUNK_TILES, N_QUERY], F32, name="s_ps")
-            for i in range(CHUNK_TILES):
+        def score_unit(u):
+            s_ps[u] = psum_s.tile([P, UNIT_TILES, N_QUERY], F32, name="s_ps")
+            for place in range(UNIT_TILES):
+                i = u * UNIT_TILES + place
                 for c in range(FEAT_PASSES):
                     nc.tensor.matmul_mx(
-                        out=s_ps[j][:, i, :],
-                        lhsT=e_codes[j][:, i, c, :].bitcast(FP8X4),
-                        lhsT_scale=e_scales[j][:, i, c, :],
+                        out=s_ps[u][:, place, :],
+                        lhsT=e_codes[i][:, c, :].bitcast(FP8X4),
+                        lhsT_scale=e_scales[i][:, c, :],
                         rhs=f_codes[:, c, :].bitcast(FP8X4),
                         rhs_scale=f_scales[:, c, :],
                         start=(c == 0),
                         stop=(c == FEAT_PASSES - 1),
                     )
-            squares[j] = chunks.tile([P, CHUNK_TILES, N_QUERY], F32, name="squares")
-            nc.scalar.activation(out=squares[j][:], in_=s_ps[j][:], func=ACT.Square)
+            squares[u] = units.tile([P, UNIT_TILES, N_QUERY], F32, name="squares")
+            nc.scalar.activation(out=squares[u][:], in_=s_ps[u][:], func=ACT.Square)
 
-        def chunk_cubes(j):
-            return cubes[:, j * CHUNK_TILES : (j + 1) * CHUNK_TILES, :]
+        def unit_cubes(u):
+            return cubes[:, u * UNIT_TILES : (u + 1) * UNIT_TILES, :]
 
-        def cube_chunk(j):
-            nc.vector.tensor_tensor(out=chunk_cubes(j), in0=s_ps[j][:], in1=squares[j][:], op=ALU.mult)
+        def cube_unit(u):
+            nc.vector.tensor_tensor(out=unit_cubes(u), in0=s_ps[u][:], in1=squares[u][:], op=ALU.mult)
+            abs_cubes[u] = units.tile([P, UNIT_TILES, N_QUERY], F32, name="abs_cubes")
+            nc.scalar.activation(out=abs_cubes[u][:], in_=unit_cubes(u), func=ACT.Abs)
 
-        def abs_chunk(j):
-            abs_cubes[j] = chunks.tile([P, CHUNK_TILES, N_QUERY], F32, name="abs_cubes")
-            nc.scalar.activation(out=abs_cubes[j][:], in_=chunk_cubes(j), func=ACT.Abs)
-
-        def sum_chunk(j):
-            for i in range(CHUNK_TILES):
-                tile_index = j * CHUNK_TILES + i
+        def sum_unit(u):
+            for place in range(UNIT_TILES):
+                i = u * UNIT_TILES + place
                 nc.tensor.matmul(
                     rowsum_ps[:],
-                    lhsT=abs_cubes[j][:, i, :],
+                    lhsT=abs_cubes[u][:, place, :],
                     rhs=ones[:],
-                    start=(tile_index == 0),
-                    stop=(tile_index == EX_TILES - 1),
+                    start=(i == 0),
+                    stop=(i == EX_TILES - 1),
                 )
 
-        for k in range(N_CHUNKS + SUM_LAG):
-            if k < N_CHUNKS:
-                transpose_chunk(k)
-            if 0 <= k - CUBE_LAG < N_CHUNKS:
-                cube_chunk(k - CUBE_LAG)
-            if k < N_CHUNKS:
-                quantise_chunk(k)
-            if 0 <= k - SCORE_LAG < N_CHUNKS:
-                score_chunk(k - SCORE_LAG)
-            if 0 <= k - CUBE_LAG < N_CHUNKS:
-                abs_chunk(k - CUBE_LAG)
-            if 0 <= k - SUM_LAG:
-                sum_chunk(k - SUM_LAG)
+        for i in range(EX_TILES):
+            transpose_tile(i)
+            if i >= 1:
+                quantise_tile(i - 1)
+        quantise_tile(EX_TILES - 1)
+
+        for u in range(N_UNITS):
+            score_unit(u)
+            if u >= 1:
+                cube_unit(u - 1)
+        cube_unit(N_UNITS - 1)
+        for u in range(N_UNITS):
+            sum_unit(u)
 
         r_grouped = keep.tile([P, EX_PASSES, N_LABEL, PACK], BF16, align_bytes=64)
         r_codes = keep.tile([P, EX_PASSES, N_LABEL], U32, align_bytes=64)
@@ -170,7 +166,7 @@ def tile_minerva_pa_s_kernel(tc, f_norm, e_norm, ex_class_reps, out):
 
         inverse = keep.tile([P, 1], F32)
         nc.vector.reciprocal(out=inverse[:], in_=rowsum_ps[:, 0:1])
-        inverse_ps = psum_norm.tile([P, N_QUERY], F32)
+        inverse_ps = psum_xt.tile([P, N_QUERY], F32, tag="xt")
         nc.tensor.transpose(inverse_ps[:], inverse[:, 0:1].to_broadcast([P, P]), identity[:])
         nc.vector.quantize_mx(
             out=r_codes[:].rearrange("p g n -> p (g n)").bitcast(FP8X4),

@@ -10,6 +10,7 @@ U8 = mybir.dt.uint8
 FP8X4 = mybir.dt.float8_e4m3fn_x4
 ALU = mybir.AluOpType
 ACT = mybir.ActivationFunctionType
+AXIS = mybir.AxisListType
 
 P = 128
 PACK = 4
@@ -24,27 +25,9 @@ EPS = 1e-12
 FEAT_PASSES = N_FEAT // K_PASS
 EX_PASSES = N_EX // K_PASS
 EX_TILES = N_EX // P
-WORD_BLOCKS = N_FEAT // 2 // P
-UNIT_TILES = 2
-N_UNITS = EX_TILES // UNIT_TILES
-SUM_COLS = 64
+UNITS = ((0, 2), (2, 2), (4, 2), (6, 1), (7, 1))
 
 FLOPS = 2 * N_QUERY * N_FEAT * N_EX + 2 * N_QUERY * N_EX * N_LABEL
-
-
-def transpose_rows(nc, psum_xt, rows, identity):
-    words = rows.bitcast(F32)
-    xt = psum_xt.tile([P, WORD_BLOCKS, P], F32)
-    for w in range(WORD_BLOCKS):
-        nc.tensor.transpose(xt[:, w, :], words[:, w * P : (w + 1) * P], identity[:])
-    return xt
-
-
-def group_features(copy, xt, grouped):
-    copy(
-        out=grouped.bitcast(F32).rearrange("p (c r u) -> p c r u", c=FEAT_PASSES, u=2),
-        in_=xt[:].rearrange("p (c u) r -> p c r u", u=2),
-    )
 
 
 def tile_minerva_pa_s_kernel(tc, f_norm, e_norm, ex_class_reps, out):
@@ -53,144 +36,223 @@ def tile_minerva_pa_s_kernel(tc, f_norm, e_norm, ex_class_reps, out):
         stack.enter_context(tc.manual_schedule())
         keep = stack.enter_context(tc.tile_pool(name="keep", bufs=1))
         tiles = stack.enter_context(tc.tile_pool(name="tiles", bufs=EX_TILES))
-        units = stack.enter_context(tc.tile_pool(name="units", bufs=N_UNITS))
-        psum_xt = stack.enter_context(tc.psum_pool(name="psum_xt", bufs=3))
-        psum_s = stack.enter_context(tc.psum_pool(name="psum_s", bufs=N_UNITS))
-        psum_sum = stack.enter_context(tc.psum_pool(name="psum_sum", bufs=1))
+        units = stack.enter_context(tc.tile_pool(name="units", bufs=len(UNITS)))
+        psum_xt = stack.enter_context(tc.psum_pool(name="psum_xt", bufs=4))
+        psum_s = stack.enter_context(tc.psum_pool(name="psum_s", bufs=4))
 
-        e_view = e_norm.rearrange("(g p t) d -> p g t d", p=P, t=PACK)
+        e_view = e_norm.rearrange("(g h m u e) d -> g u h m e d", g=EX_PASSES, h=2, u=2, e=2)
         r_view = ex_class_reps.rearrange("(g p t) n -> p g t n", p=P, t=PACK)
 
         f_rows = keep.tile([P, N_FEAT], BF16)
         nc.sync.dma_start(out=f_rows[:], in_=f_norm)
         e_rows = []
-        for g in range(EX_PASSES):
-            for t in range(PACK):
-                e_tile = tiles.tile([P, N_FEAT], BF16, name="e_tile")
-                nc.sync.dma_start(out=e_tile[:], in_=e_view[:, g, t, :])
-                e_rows.append(e_tile)
+        for i in range(EX_TILES):
+            e_tile = tiles.tile([P, N_FEAT], BF16, name="e_tile")
+            nc.sync.dma_start(out=e_tile[:], in_=e_view[i // 4, i // 2 % 2, i % 2])
+            e_rows.append(e_tile)
         r_rows = keep.tile([P, EX_PASSES, PACK, N_LABEL], BF16)
         nc.sync.dma_start(out=r_rows[:], in_=r_view)
 
         identity = keep.tile([P, P], F32)
         make_identity(nc, identity[:])
-        ones = keep.tile([P, SUM_COLS], F32)
+        ones = keep.tile([P, 1], F32)
         nc.vector.memset(ones[:], 1.0)
         table_warm = keep.tile([P, 1], F32)
-        nc.scalar.activation(out=table_warm[:], in_=ones[:, 0:1], func=ACT.Abs)
+        nc.scalar.activation(out=table_warm[:], in_=ones[:], func=ACT.Abs)
+
+        def transpose_words(rows, first, count):
+            words = rows.bitcast(F32)
+            xt = psum_xt.tile([P, count, P], F32, name="xt")
+            for w in range(count):
+                nc.tensor.transpose(xt[:, w, :], words[:, (first + w) * P : (first + w + 1) * P], identity[:])
+            return xt
+
+        def group_words(copy, xt, grouped):
+            copy(
+                out=grouped.bitcast(F32).rearrange("p (c r u) -> p c r u", r=P, u=2),
+                in_=xt[:].rearrange("p (c u) r -> p c r u", u=2),
+            )
 
         f_grouped = keep.tile([P, N_FEAT], BF16, align_bytes=64)
         f_codes = keep.tile([P, FEAT_PASSES, N_QUERY], U32, align_bytes=64)
         f_scales = keep.tile([P, FEAT_PASSES, N_QUERY], U8, align_bytes=64)
-        f_xt = transpose_rows(nc, psum_xt, f_rows[:], identity)
-        group_features(nc.scalar.copy, f_xt, f_grouped[:])
-        nc.vector.quantize_mx(
-            out=f_codes[:].rearrange("p c q -> p (c q)").bitcast(FP8X4),
-            scales=f_scales[:].rearrange("p c q -> p (c q)"),
-            in_=f_grouped[:],
-        )
 
-        cubes = keep.tile([P, EX_TILES, N_QUERY], F32)
-        rowsum_ps = psum_sum.tile([P, SUM_COLS], F32)
-        e_grouped, e_codes, e_scales, s_ps, squares, abs_cubes = {}, {}, {}, {}, {}, {}
+        a = keep.tile([P, N_EX], F32)
+        parts = keep.tile([P, len(UNITS)], F32)
+        e_xt, e_grouped, e_codes, e_scales, s_ps, squares = {}, {}, {}, {}, {}, {}
 
         def transpose_tile(i):
-            e_xt = transpose_rows(nc, psum_xt, e_rows[i][:], identity)
             e_grouped[i] = tiles.tile([P, N_FEAT], BF16, name="e_grouped", align_bytes=64)
-            copy = nc.vector.tensor_copy if i % 3 == 2 else nc.scalar.copy
-            group_features(copy, e_xt, e_grouped[i][:])
-
-        def quantise_tile(i):
             e_codes[i] = tiles.tile([P, FEAT_PASSES, P], U32, name="e_codes", align_bytes=64)
             e_scales[i] = tiles.tile([P, FEAT_PASSES, P], U8, name="e_scales", align_bytes=64)
+            e_xt[i] = transpose_words(e_rows[i][:], 0, 4)
+
+        def copy_tile(i, copy):
+            group_words(copy, e_xt[i], e_grouped[i][:])
+
+        def quantise_tile(i):
             nc.vector.quantize_mx(
                 out=e_codes[i][:].rearrange("p c x -> p (c x)").bitcast(FP8X4),
                 scales=e_scales[i][:].rearrange("p c x -> p (c x)"),
                 in_=e_grouped[i][:],
             )
 
-        def score_unit(u):
-            s_ps[u] = psum_s.tile([P, UNIT_TILES, N_QUERY], F32, name="s_ps")
-            for place in range(UNIT_TILES):
-                i = u * UNIT_TILES + place
-                for c in range(FEAT_PASSES):
-                    nc.tensor.matmul_mx(
-                        out=s_ps[u][:, place, :],
-                        lhsT=e_codes[i][:, c, :].bitcast(FP8X4),
-                        lhsT_scale=e_scales[i][:, c, :],
-                        rhs=f_codes[:, c, :].bitcast(FP8X4),
-                        rhs_scale=f_scales[:, c, :],
-                        start=(c == 0),
-                        stop=(c == FEAT_PASSES - 1),
-                    )
-            squares[u] = units.tile([P, UNIT_TILES, N_QUERY], F32, name="squares")
-            nc.scalar.activation(out=squares[u][:], in_=s_ps[u][:], func=ACT.Square)
-
-        def unit_cubes(u):
-            return cubes[:, u * UNIT_TILES : (u + 1) * UNIT_TILES, :]
-
-        def cube_unit(u):
-            nc.vector.tensor_tensor(out=unit_cubes(u), in0=s_ps[u][:], in1=squares[u][:], op=ALU.mult)
-            abs_cubes[u] = units.tile([P, UNIT_TILES, N_QUERY], F32, name="abs_cubes")
-            nc.scalar.activation(out=abs_cubes[u][:], in_=unit_cubes(u), func=ACT.Abs)
-
-        def sum_unit(u):
-            for place in range(UNIT_TILES):
-                i = u * UNIT_TILES + place
-                nc.tensor.matmul(
-                    rowsum_ps[:],
-                    lhsT=abs_cubes[u][:, place, :],
-                    rhs=ones[:],
-                    start=(i == 0),
-                    stop=(i == EX_TILES - 1),
+        def score_tile(u, i):
+            first, count = UNITS[u]
+            if i == first:
+                s_ps[u] = psum_s.tile([P, count, P], F32, name="s_ps")
+            for c in range(FEAT_PASSES):
+                nc.tensor.matmul_mx(
+                    out=s_ps[u][:, i - first, :],
+                    lhsT=f_codes[:, c, :].bitcast(FP8X4),
+                    lhsT_scale=f_scales[:, c, :],
+                    rhs=e_codes[i][:, c, :].bitcast(FP8X4),
+                    rhs_scale=e_scales[i][:, c, :],
+                    start=(c == 0),
+                    stop=(c == FEAT_PASSES - 1),
                 )
 
-        for i in range(EX_TILES):
-            transpose_tile(i)
-            if i >= 1:
-                quantise_tile(i - 1)
-        quantise_tile(EX_TILES - 1)
+        def score_unit(u):
+            first, count = UNITS[u]
+            for i in range(first, first + count):
+                score_tile(u, i)
 
-        for u in range(N_UNITS):
-            score_unit(u)
-            if u >= 1:
-                cube_unit(u - 1)
-        cube_unit(N_UNITS - 1)
-        for u in range(N_UNITS):
-            sum_unit(u)
+        def square_unit(u):
+            squares[u] = units.tile([P, UNITS[u][1], P], F32, name="squares")
+            nc.scalar.activation(out=squares[u][:], in_=s_ps[u][:], func=ACT.Square)
+
+        def unit_a(u):
+            first, count = UNITS[u]
+            return a[:, first * P : (first + count) * P]
+
+        def cube_unit(u):
+            nc.vector.tensor_tensor(
+                out=unit_a(u),
+                in0=s_ps[u][:].rearrange("p t x -> p (t x)"),
+                in1=squares[u][:].rearrange("p t x -> p (t x)"),
+                op=ALU.mult,
+            )
+
+        def sum_unit(u):
+            abs_a = units.tile([P, UNITS[u][1] * P], F32, name="abs_a")
+            nc.scalar.activation(out=abs_a[:], in_=unit_a(u), func=ACT.Abs, accum_out=parts[:, u : u + 1])
+
+        vec, sca = nc.vector.tensor_copy, nc.scalar.copy
+        last = EX_TILES - 1
+        half = N_FEAT // 2
+        f_xt = transpose_words(f_rows[:], 0, 4)
+        group_words(vec, f_xt, f_grouped[:])
+        transpose_tile(0)
+        copy_tile(0, sca)
+        nc.vector.quantize_mx(
+            out=f_codes[:].rearrange("p c q -> p (c q)").bitcast(FP8X4),
+            scales=f_scales[:].rearrange("p c q -> p (c q)"),
+            in_=f_grouped[:],
+        )
+        transpose_tile(1)
+        copy_tile(1, sca)
+        quantise_tile(0)
+        transpose_tile(2)
+        copy_tile(2, vec)
+        quantise_tile(1)
+        transpose_tile(3)
+        copy_tile(3, sca)
+        quantise_tile(2)
+        score_tile(0, 0)
+        transpose_tile(4)
+        copy_tile(4, sca)
+        quantise_tile(3)
+        score_tile(0, 1)
+        square_unit(0)
+        cube_unit(0)
+        transpose_tile(5)
+        copy_tile(5, sca)
+        quantise_tile(4)
+        score_tile(1, 2)
+        transpose_tile(6)
+        copy_tile(6, sca)
+        quantise_tile(5)
+        score_tile(1, 3)
+        square_unit(1)
+
+        e_grouped[last] = tiles.tile([P, N_FEAT], BF16, name="e_grouped", align_bytes=64)
+        e_codes[last] = tiles.tile([P, FEAT_PASSES, P], U32, name="e_codes", align_bytes=64)
+        e_scales[last] = tiles.tile([P, FEAT_PASSES, P], U8, name="e_scales", align_bytes=64)
+        halves = [transpose_words(e_rows[last][:], 2 * c, 2) for c in range(FEAT_PASSES)]
+        group_words(sca, halves[0], e_grouped[last][:, :half])
+        group_words(vec, halves[1], e_grouped[last][:, half:])
+        cube_unit(1)
+        sum_unit(0)
+        quantise_tile(6)
+        for c in range(FEAT_PASSES):
+            nc.vector.quantize_mx(
+                out=e_codes[last][:, c, :].bitcast(FP8X4),
+                scales=e_scales[last][:, c, :],
+                in_=e_grouped[last][:, c * half : (c + 1) * half],
+            )
+        score_unit(2)
+        square_unit(2)
+        score_unit(3)
+        square_unit(3)
+        cube_unit(2)
+        sum_unit(1)
+        cube_unit(3)
+        score_unit(4)
+        square_unit(4)
+        sum_unit(2)
+        sum_unit(3)
 
         r_grouped = keep.tile([P, EX_PASSES, N_LABEL, PACK], BF16, align_bytes=64)
         r_codes = keep.tile([P, EX_PASSES, N_LABEL], U32, align_bytes=64)
         r_scales = keep.tile([P, EX_PASSES, N_LABEL], U8, align_bytes=64)
         nc.vector.tensor_copy(out=r_grouped[:], in_=r_rows[:].rearrange("p g t n -> p g n t"))
+        cube_unit(4)
+        nc.vector.tensor_reduce(
+            out=parts[:, len(UNITS) - 1 : len(UNITS)],
+            in_=unit_a(4),
+            axis=AXIS.X,
+            op=ALU.add,
+            apply_absolute_value=True,
+        )
 
+        early = keep.tile([P, 1], F32)
+        nc.vector.reduce_sum(out=early[:], in_=parts[:, : len(UNITS) - 1], axis=AXIS.X)
+        total = keep.tile([P, 1], F32)
         inverse = keep.tile([P, 1], F32)
-        nc.vector.reciprocal(out=inverse[:], in_=rowsum_ps[:, 0:1])
-        inverse_ps = psum_xt.tile([P, N_QUERY], F32, tag="xt")
-        nc.tensor.transpose(inverse_ps[:], inverse[:, 0:1].to_broadcast([P, P]), identity[:])
+        nc.vector.tensor_scalar(
+            out=total[:],
+            in0=parts[:, len(UNITS) - 1 : len(UNITS)],
+            scalar1=early[:, 0:1],
+            scalar2=EPS,
+            op0=ALU.add,
+            op1=ALU.max,
+        )
+        nc.vector.reciprocal(out=inverse[:], in_=total[:])
+
+        p_rows = keep.tile([P, N_EX], BF16, align_bytes=64)
+        nc.vector.tensor_scalar(
+            out=p_rows[:, :512], in0=a[:, :512], scalar1=inverse[:, 0:1], scalar2=None, op0=ALU.mult
+        )
+        nc.scalar.activation(out=p_rows[:, 512:768], in_=a[:, 512:768], func=ACT.Copy, scale=inverse[:, 0:1])
+        nc.vector.tensor_scalar(
+            out=p_rows[:, 768:], in0=a[:, 768:], scalar1=inverse[:, 0:1], scalar2=None, op0=ALU.mult
+        )
+        p_grouped = keep.tile([P, EX_PASSES, N_QUERY * PACK], BF16, align_bytes=64)
+        p_codes = keep.tile([P, EX_PASSES, N_QUERY], U32, align_bytes=64)
+        p_scales = keep.tile([P, EX_PASSES, N_QUERY], U8, align_bytes=64)
         nc.vector.quantize_mx(
             out=r_codes[:].rearrange("p g n -> p (g n)").bitcast(FP8X4),
             scales=r_scales[:].rearrange("p g n -> p (g n)"),
             in_=r_grouped[:].rearrange("p g n t -> p (g n t)"),
         )
-
-        p_grouped = keep.tile([P, EX_PASSES, N_QUERY, PACK], BF16, align_bytes=64)
-        p_codes = keep.tile([P, EX_PASSES, N_QUERY], U32, align_bytes=64)
-        p_scales = keep.tile([P, EX_PASSES, N_QUERY], U8, align_bytes=64)
-        for g in range(EX_PASSES):
-            nc.vector.scalar_tensor_tensor(
-                out=p_grouped[:, g, :, :],
-                in0=inverse_ps[:].unsqueeze(2).to_broadcast([P, N_QUERY, PACK]),
-                scalar=1.0 / EPS,
-                in1=cubes[:, g * PACK : (g + 1) * PACK, :].rearrange("p t q -> p q t"),
-                op0=ALU.min,
-                op1=ALU.mult,
-            )
+        p_xt = [transpose_words(p_rows[:], 2 * g, 2) for g in range(EX_PASSES)]
+        group_words(nc.scalar.copy, p_xt[0], p_grouped[:, 0, :])
+        group_words(nc.vector.tensor_copy, p_xt[1], p_grouped[:, 1, :])
         for g in range(EX_PASSES):
             nc.vector.quantize_mx(
                 out=p_codes[:, g, :].bitcast(FP8X4),
                 scales=p_scales[:, g, :],
-                in_=p_grouped[:, g, :, :].rearrange("p q t -> p (q t)"),
+                in_=p_grouped[:, g, :],
             )
 
         echo_ps = psum_s.tile([P, N_LABEL], F32, tag="s_ps")

@@ -27,6 +27,8 @@ EX_PASSES = N_EX // K_PASS
 EX_TILES = N_EX // P
 UNITS = ((0, 2), (2, 2), (4, 2), (6, 1), (7, 1))
 
+IDLE_PASSES = 10
+
 FLOPS = 2 * N_QUERY * N_FEAT * N_EX + 2 * N_QUERY * N_EX * N_LABEL
 
 
@@ -37,8 +39,8 @@ def tile_minerva_pa_s_kernel(tc, f_norm, e_norm, ex_class_reps, out):
         keep = stack.enter_context(tc.tile_pool(name="keep", bufs=1))
         tiles = stack.enter_context(tc.tile_pool(name="tiles", bufs=EX_TILES))
         units = stack.enter_context(tc.tile_pool(name="units", bufs=len(UNITS)))
-        psum_xt = stack.enter_context(tc.psum_pool(name="psum_xt", bufs=4))
-        psum_s = stack.enter_context(tc.psum_pool(name="psum_s", bufs=4))
+        psum_xt = stack.enter_context(tc.psum_pool(name="psum_xt", bufs=3))
+        psum_s = stack.enter_context(tc.psum_pool(name="psum_s", bufs=len(UNITS)))
 
         e_view = e_norm.rearrange("(g h m u e) d -> g u h m e d", g=EX_PASSES, h=2, u=2, e=2)
         r_view = ex_class_reps.rearrange("(g p t) n -> p g t n", p=P, t=PACK)
@@ -141,82 +143,75 @@ def tile_minerva_pa_s_kernel(tc, f_norm, e_norm, ex_class_reps, out):
         last = EX_TILES - 1
         half = N_FEAT // 2
         f_xt = transpose_words(f_rows[:], 0, 4)
-        group_words(vec, f_xt, f_grouped[:])
-        transpose_tile(0)
-        copy_tile(0, sca)
+        group_words(sca, f_xt, f_grouped[:])
         nc.vector.quantize_mx(
             out=f_codes[:].rearrange("p c q -> p (c q)").bitcast(FP8X4),
             scales=f_scales[:].rearrange("p c q -> p (c q)"),
             in_=f_grouped[:],
         )
-        transpose_tile(1)
-        copy_tile(1, sca)
-        quantise_tile(0)
-        transpose_tile(2)
-        copy_tile(2, vec)
-        quantise_tile(1)
-        transpose_tile(3)
-        copy_tile(3, sca)
-        quantise_tile(2)
-        score_tile(0, 0)
-        transpose_tile(4)
-        copy_tile(4, sca)
-        quantise_tile(3)
-        score_tile(0, 1)
-        square_unit(0)
-        cube_unit(0)
-        transpose_tile(5)
-        copy_tile(5, sca)
-        quantise_tile(4)
-        score_tile(1, 2)
-        transpose_tile(6)
-        copy_tile(6, sca)
-        quantise_tile(5)
-        score_tile(1, 3)
-        square_unit(1)
-
+        for i in range(last):
+            transpose_tile(i)
+            copy_tile(i, vec if i % 3 == 2 else sca)
+            if i >= 1:
+                quantise_tile(i - 1)
         e_grouped[last] = tiles.tile([P, N_FEAT], BF16, name="e_grouped", align_bytes=64)
         e_codes[last] = tiles.tile([P, FEAT_PASSES, P], U32, name="e_codes", align_bytes=64)
         e_scales[last] = tiles.tile([P, FEAT_PASSES, P], U8, name="e_scales", align_bytes=64)
         halves = [transpose_words(e_rows[last][:], 2 * c, 2) for c in range(FEAT_PASSES)]
         group_words(sca, halves[0], e_grouped[last][:, :half])
         group_words(vec, halves[1], e_grouped[last][:, half:])
-        cube_unit(1)
-        sum_unit(0)
-        quantise_tile(6)
+        quantise_tile(last - 1)
         for c in range(FEAT_PASSES):
             nc.vector.quantize_mx(
                 out=e_codes[last][:, c, :].bitcast(FP8X4),
                 scales=e_scales[last][:, c, :],
                 in_=e_grouped[last][:, c * half : (c + 1) * half],
             )
-        score_unit(2)
-        square_unit(2)
-        score_unit(3)
-        square_unit(3)
-        cube_unit(2)
-        sum_unit(1)
-        cube_unit(3)
-        score_unit(4)
-        square_unit(4)
-        sum_unit(2)
-        sum_unit(3)
 
         r_grouped = keep.tile([P, EX_PASSES, N_LABEL, PACK], BF16, align_bytes=64)
         r_codes = keep.tile([P, EX_PASSES, N_LABEL], U32, align_bytes=64)
         r_scales = keep.tile([P, EX_PASSES, N_LABEL], U8, align_bytes=64)
-        nc.vector.tensor_copy(out=r_grouped[:], in_=r_rows[:].rearrange("p g t n -> p g n t"))
-        cube_unit(4)
-        nc.vector.tensor_reduce(
-            out=parts[:, len(UNITS) - 1 : len(UNITS)],
-            in_=unit_a(4),
-            axis=AXIS.X,
-            op=ALU.add,
-            apply_absolute_value=True,
-        )
 
+        def regroup_reps(g):
+            nc.vector.tensor_copy(out=r_grouped[:, g, :, :], in_=r_rows[:, g, :, :].rearrange("p t n -> p n t"))
+
+        def reduce_unit(u):
+            nc.vector.tensor_reduce(
+                out=parts[:, u : u + 1], in_=unit_a(u), axis=AXIS.X, op=ALU.add, apply_absolute_value=True
+            )
+
+        for u in range(len(UNITS)):
+            score_unit(u)
+        idle_ps = psum_xt.tile([P, FEAT_PASSES * N_QUERY], F32, tag="xt")
+        for k in range(IDLE_PASSES):
+            nc.tensor.matmul_mx(
+                out=idle_ps[:],
+                lhsT=f_codes[:, 0, :].bitcast(FP8X4),
+                lhsT_scale=f_scales[:, 0, :],
+                rhs=f_codes[:].rearrange("p c q -> p (c q)").bitcast(FP8X4),
+                rhs_scale=f_scales[:].rearrange("p c q -> p (c q)"),
+                start=True,
+                stop=True,
+            )
+        square_unit(0)
+        square_unit(1)
+        cube_unit(0)
+        cube_unit(1)
+        square_unit(2)
+        cube_unit(2)
+        sum_unit(0)
+        square_unit(3)
+        cube_unit(3)
+        square_unit(4)
+        sum_unit(1)
+        sum_unit(3)
+        reduce_unit(2)
+        regroup_reps(0)
+        cube_unit(4)
         early = keep.tile([P, 1], F32)
         nc.vector.reduce_sum(out=early[:], in_=parts[:, : len(UNITS) - 1], axis=AXIS.X)
+        reduce_unit(4)
+
         total = keep.tile([P, 1], F32)
         inverse = keep.tile([P, 1], F32)
         nc.vector.tensor_scalar(
@@ -237,17 +232,18 @@ def tile_minerva_pa_s_kernel(tc, f_norm, e_norm, ex_class_reps, out):
         nc.vector.tensor_scalar(
             out=p_rows[:, 768:], in0=a[:, 768:], scalar1=inverse[:, 0:1], scalar2=None, op0=ALU.mult
         )
-        p_grouped = keep.tile([P, EX_PASSES, N_QUERY * PACK], BF16, align_bytes=64)
-        p_codes = keep.tile([P, EX_PASSES, N_QUERY], U32, align_bytes=64)
-        p_scales = keep.tile([P, EX_PASSES, N_QUERY], U8, align_bytes=64)
+        regroup_reps(1)
         nc.vector.quantize_mx(
             out=r_codes[:].rearrange("p g n -> p (g n)").bitcast(FP8X4),
             scales=r_scales[:].rearrange("p g n -> p (g n)"),
             in_=r_grouped[:].rearrange("p g n t -> p (g n t)"),
         )
+        p_grouped = keep.tile([P, EX_PASSES, N_QUERY * PACK], BF16, align_bytes=64)
+        p_codes = keep.tile([P, EX_PASSES, N_QUERY], U32, align_bytes=64)
+        p_scales = keep.tile([P, EX_PASSES, N_QUERY], U8, align_bytes=64)
         p_xt = [transpose_words(p_rows[:], 2 * g, 2) for g in range(EX_PASSES)]
-        group_words(nc.scalar.copy, p_xt[0], p_grouped[:, 0, :])
-        group_words(nc.vector.tensor_copy, p_xt[1], p_grouped[:, 1, :])
+        for g in range(EX_PASSES):
+            group_words(sca, p_xt[g], p_grouped[:, g, :])
         for g in range(EX_PASSES):
             nc.vector.quantize_mx(
                 out=p_codes[:, g, :].bitcast(FP8X4),

@@ -25,7 +25,7 @@ EPS = 1e-12
 FEAT_PASSES = N_FEAT // K_PASS
 EX_PASSES = N_EX // K_PASS
 EX_TILES = N_EX // P
-UNITS = ((0, 2), (2, 2), (4, 2), (6, 1), (7, 1))
+UNITS = ((0, 2), (2, 2), (4, 3), (7, 1))
 
 IDLE_PASSES = 10
 
@@ -39,8 +39,8 @@ def tile_minerva_pa_s_kernel(tc, f_norm, e_norm, ex_class_reps, out):
         keep = stack.enter_context(tc.tile_pool(name="keep", bufs=1))
         tiles = stack.enter_context(tc.tile_pool(name="tiles", bufs=EX_TILES))
         units = stack.enter_context(tc.tile_pool(name="units", bufs=len(UNITS)))
-        psum_xt = stack.enter_context(tc.psum_pool(name="psum_xt", bufs=3))
-        psum_s = stack.enter_context(tc.psum_pool(name="psum_s", bufs=len(UNITS)))
+        psum_xt = stack.enter_context(tc.psum_pool(name="psum_xt", bufs=4))
+        psum_s = stack.enter_context(tc.psum_pool(name="psum_s", bufs=4))
 
         e_view = e_norm.rearrange("(g h m u e) d -> g u h m e d", g=EX_PASSES, h=2, u=2, e=2)
         r_view = ex_class_reps.rearrange("(g p t) n -> p g t n", p=P, t=PACK)
@@ -57,10 +57,10 @@ def tile_minerva_pa_s_kernel(tc, f_norm, e_norm, ex_class_reps, out):
 
         identity = keep.tile([P, P], F32)
         make_identity(nc, identity[:])
-        ones = keep.tile([P, 1], F32)
+        ones = keep.tile([P, P], F32)
         nc.vector.memset(ones[:], 1.0)
         table_warm = keep.tile([P, 1], F32)
-        nc.scalar.activation(out=table_warm[:], in_=ones[:], func=ACT.Abs)
+        nc.scalar.activation(out=table_warm[:], in_=ones[:, 0:1], func=ACT.Abs)
 
         def transpose_words(rows, first, count):
             words = rows.bitcast(F32)
@@ -142,6 +142,13 @@ def tile_minerva_pa_s_kernel(tc, f_norm, e_norm, ex_class_reps, out):
         vec, sca = nc.vector.tensor_copy, nc.scalar.copy
         last = EX_TILES - 1
         half = N_FEAT // 2
+        warm_ps = psum_s.tile([P, P], F32, tag="s_ps")
+
+        def warm():
+            nc.tensor.matmul(warm_ps[:], lhsT=ones[:], rhs=ones[:], start=True, stop=True)
+
+        for k in range(3):
+            warm()
         f_xt = transpose_words(f_rows[:], 0, 4)
         group_words(sca, f_xt, f_grouped[:])
         nc.vector.quantize_mx(
@@ -152,6 +159,8 @@ def tile_minerva_pa_s_kernel(tc, f_norm, e_norm, ex_class_reps, out):
         for i in range(last):
             transpose_tile(i)
             copy_tile(i, vec if i % 3 == 2 else sca)
+            if i % 2 == 0:
+                warm()
             if i >= 1:
                 quantise_tile(i - 1)
         e_grouped[last] = tiles.tile([P, N_FEAT], BF16, name="e_grouped", align_bytes=64)
@@ -172,8 +181,12 @@ def tile_minerva_pa_s_kernel(tc, f_norm, e_norm, ex_class_reps, out):
         r_codes = keep.tile([P, EX_PASSES, N_LABEL], U32, align_bytes=64)
         r_scales = keep.tile([P, EX_PASSES, N_LABEL], U8, align_bytes=64)
 
-        def regroup_reps(g):
-            nc.vector.tensor_copy(out=r_grouped[:, g, :, :], in_=r_rows[:, g, :, :].rearrange("p t n -> p n t"))
+        def regroup_reps(quarter):
+            g, n = quarter // 2, N_LABEL // 2 * (quarter % 2)
+            labels = slice(n, n + N_LABEL // 2)
+            nc.vector.tensor_copy(
+                out=r_grouped[:, g, labels, :], in_=r_rows[:, g, :, labels].rearrange("p t n -> p n t")
+            )
 
         def reduce_unit(u):
             nc.vector.tensor_reduce(
@@ -198,22 +211,19 @@ def tile_minerva_pa_s_kernel(tc, f_norm, e_norm, ex_class_reps, out):
         cube_unit(0)
         cube_unit(1)
         square_unit(2)
-        cube_unit(2)
-        sum_unit(0)
         square_unit(3)
+        cube_unit(2)
         cube_unit(3)
-        square_unit(4)
-        sum_unit(1)
-        sum_unit(3)
-        reduce_unit(2)
-        regroup_reps(0)
-        cube_unit(4)
-        early = keep.tile([P, 1], F32)
-        nc.vector.reduce_sum(out=early[:], in_=parts[:, : len(UNITS) - 1], axis=AXIS.X)
-        reduce_unit(4)
+        sum_unit(0)
+        sum_unit(2)
+        reduce_unit(1)
+        reduce_unit(3)
 
+        early = keep.tile([P, 1], F32)
         total = keep.tile([P, 1], F32)
         inverse = keep.tile([P, 1], F32)
+        nc.vector.reduce_sum(out=early[:], in_=parts[:, : len(UNITS) - 1], axis=AXIS.X)
+        regroup_reps(0)
         nc.vector.tensor_scalar(
             out=total[:],
             in0=parts[:, len(UNITS) - 1 : len(UNITS)],
@@ -222,7 +232,9 @@ def tile_minerva_pa_s_kernel(tc, f_norm, e_norm, ex_class_reps, out):
             op0=ALU.add,
             op1=ALU.max,
         )
+        regroup_reps(1)
         nc.vector.reciprocal(out=inverse[:], in_=total[:])
+        regroup_reps(2)
 
         p_rows = keep.tile([P, N_EX], BF16, align_bytes=64)
         nc.vector.tensor_scalar(
@@ -232,7 +244,7 @@ def tile_minerva_pa_s_kernel(tc, f_norm, e_norm, ex_class_reps, out):
         nc.vector.tensor_scalar(
             out=p_rows[:, 768:], in0=a[:, 768:], scalar1=inverse[:, 0:1], scalar2=None, op0=ALU.mult
         )
-        regroup_reps(1)
+        regroup_reps(3)
         nc.vector.quantize_mx(
             out=r_codes[:].rearrange("p g n -> p (g n)").bitcast(FP8X4),
             scales=r_scales[:].rearrange("p g n -> p (g n)"),

@@ -25,9 +25,9 @@ EPS = 1e-12
 FEAT_PASSES = N_FEAT // K_PASS
 EX_PASSES = N_EX // K_PASS
 EX_TILES = N_EX // P
-UNITS = ((0, 2), (2, 2), (4, 3), (7, 1))
+UNITS = ((0, 3), (3, 3), (6, 2))
 
-IDLE_PASSES = 10
+IDLE_PASSES = 5
 
 FLOPS = 2 * N_QUERY * N_FEAT * N_EX + 2 * N_QUERY * N_EX * N_LABEL
 
@@ -39,8 +39,8 @@ def tile_minerva_pa_s_kernel(tc, f_norm, e_norm, ex_class_reps, out):
         keep = stack.enter_context(tc.tile_pool(name="keep", bufs=1))
         tiles = stack.enter_context(tc.tile_pool(name="tiles", bufs=EX_TILES))
         units = stack.enter_context(tc.tile_pool(name="units", bufs=len(UNITS)))
-        psum_xt = stack.enter_context(tc.psum_pool(name="psum_xt", bufs=4))
-        psum_s = stack.enter_context(tc.psum_pool(name="psum_s", bufs=4))
+        psum_xt = stack.enter_context(tc.psum_pool(name="psum_xt", bufs=5))
+        psum_s = stack.enter_context(tc.psum_pool(name="psum_s", bufs=len(UNITS)))
 
         e_view = e_norm.rearrange("(g h m u e) d -> g u h m e d", g=EX_PASSES, h=2, u=2, e=2)
         r_view = ex_class_reps.rearrange("(g p t) n -> p g t n", p=P, t=PACK)
@@ -80,7 +80,7 @@ def tile_minerva_pa_s_kernel(tc, f_norm, e_norm, ex_class_reps, out):
         f_scales = keep.tile([P, FEAT_PASSES, N_QUERY], U8, align_bytes=64)
 
         a = keep.tile([P, N_EX], F32)
-        parts = keep.tile([P, len(UNITS)], F32)
+        parts = keep.tile([P, 2], F32)
         e_xt, e_grouped, e_codes, e_scales, s_ps, squares = {}, {}, {}, {}, {}, {}
 
         def transpose_tile(i):
@@ -135,10 +135,6 @@ def tile_minerva_pa_s_kernel(tc, f_norm, e_norm, ex_class_reps, out):
                 op=ALU.mult,
             )
 
-        def sum_unit(u):
-            abs_a = units.tile([P, UNITS[u][1] * P], F32, name="abs_a")
-            nc.scalar.activation(out=abs_a[:], in_=unit_a(u), func=ACT.Abs, accum_out=parts[:, u : u + 1])
-
         vec, sca = nc.vector.tensor_copy, nc.scalar.copy
         last = EX_TILES - 1
         half = N_FEAT // 2
@@ -158,9 +154,11 @@ def tile_minerva_pa_s_kernel(tc, f_norm, e_norm, ex_class_reps, out):
         )
         for i in range(last):
             transpose_tile(i)
-            copy_tile(i, vec if i % 3 == 2 else sca)
-            if i % 2 == 0:
+            copy_tile(i, vec if i == 2 else sca)
+            if i in (0, 2, 4):
                 warm()
+            if i == 6:
+                score_unit(0)
             if i >= 1:
                 quantise_tile(i - 1)
         e_grouped[last] = tiles.tile([P, N_FEAT], BF16, name="e_grouped", align_bytes=64)
@@ -188,63 +186,56 @@ def tile_minerva_pa_s_kernel(tc, f_norm, e_norm, ex_class_reps, out):
                 out=r_grouped[:, g, labels, :], in_=r_rows[:, g, :, labels].rearrange("p t n -> p n t")
             )
 
-        def reduce_unit(u):
-            nc.vector.tensor_reduce(
-                out=parts[:, u : u + 1], in_=unit_a(u), axis=AXIS.X, op=ALU.add, apply_absolute_value=True
-            )
-
-        for u in range(len(UNITS)):
+        for u in range(1, len(UNITS)):
             score_unit(u)
         idle_ps = psum_xt.tile([P, FEAT_PASSES * N_QUERY], F32, tag="xt")
-        for k in range(IDLE_PASSES):
-            nc.tensor.matmul_mx(
-                out=idle_ps[:],
-                lhsT=f_codes[:, 0, :].bitcast(FP8X4),
-                lhsT_scale=f_scales[:, 0, :],
-                rhs=f_codes[:].rearrange("p c q -> p (c q)").bitcast(FP8X4),
-                rhs_scale=f_scales[:].rearrange("p c q -> p (c q)"),
-                start=True,
-                stop=True,
-            )
-        square_unit(0)
-        square_unit(1)
-        cube_unit(0)
-        cube_unit(1)
-        square_unit(2)
-        square_unit(3)
-        cube_unit(2)
-        cube_unit(3)
-        sum_unit(0)
-        sum_unit(2)
-        reduce_unit(1)
-        reduce_unit(3)
 
-        early = keep.tile([P, 1], F32)
-        total = keep.tile([P, 1], F32)
-        inverse = keep.tile([P, 1], F32)
-        nc.vector.reduce_sum(out=early[:], in_=parts[:, : len(UNITS) - 1], axis=AXIS.X)
+        def idle():
+            for k in range(IDLE_PASSES):
+                nc.tensor.matmul_mx(
+                    out=idle_ps[:],
+                    lhsT=f_codes[:, 0, :].bitcast(FP8X4),
+                    lhsT_scale=f_scales[:, 0, :],
+                    rhs=f_codes[:].rearrange("p c q -> p (c q)").bitcast(FP8X4),
+                    rhs_scale=f_scales[:].rearrange("p c q -> p (c q)"),
+                    start=True,
+                    stop=True,
+                )
+
+        idle()
+        for u in range(len(UNITS)):
+            square_unit(u)
+        for u in range(len(UNITS)):
+            cube_unit(u)
+        nc.tensor.matmul(idle_ps[:, :P], lhsT=a[:, last * P :], rhs=ones[:], start=True, stop=True)
+        idle()
+
+        split = UNITS[-1][0] * P
+        abs_a = keep.tile([P, split], F32)
+        nc.scalar.activation(out=abs_a[:], in_=a[:, :split], func=ACT.Abs, accum_out=parts[:, 0:1])
         regroup_reps(0)
-        nc.vector.tensor_scalar(
-            out=total[:],
-            in0=parts[:, len(UNITS) - 1 : len(UNITS)],
-            scalar1=early[:, 0:1],
-            scalar2=EPS,
-            op0=ALU.add,
-            op1=ALU.max,
+        nc.vector.tensor_reduce(
+            out=parts[:, 1:2], in_=a[:, split:], axis=AXIS.X, op=ALU.add, apply_absolute_value=True
         )
         regroup_reps(1)
-        nc.vector.reciprocal(out=inverse[:], in_=total[:])
+
+        total = keep.tile([P, 1], F32)
+        inverse = keep.tile([P, 1], F32)
+        nc.vector.tensor_scalar(
+            out=total[:], in0=parts[:, 1:2], scalar1=parts[:, 0:1], scalar2=EPS, op0=ALU.add, op1=ALU.max
+        )
         regroup_reps(2)
+        nc.vector.reciprocal(out=inverse[:], in_=total[:])
+        regroup_reps(3)
 
         p_rows = keep.tile([P, N_EX], BF16, align_bytes=64)
         nc.vector.tensor_scalar(
-            out=p_rows[:, :512], in0=a[:, :512], scalar1=inverse[:, 0:1], scalar2=None, op0=ALU.mult
+            out=p_rows[:, :256], in0=a[:, :256], scalar1=inverse[:, 0:1], scalar2=None, op0=ALU.mult
         )
-        nc.scalar.activation(out=p_rows[:, 512:768], in_=a[:, 512:768], func=ACT.Copy, scale=inverse[:, 0:1])
+        nc.scalar.activation(out=p_rows[:, 256:512], in_=a[:, 256:512], func=ACT.Copy, scale=inverse[:, 0:1])
         nc.vector.tensor_scalar(
-            out=p_rows[:, 768:], in0=a[:, 768:], scalar1=inverse[:, 0:1], scalar2=None, op0=ALU.mult
+            out=p_rows[:, 512:], in0=a[:, 512:], scalar1=inverse[:, 0:1], scalar2=None, op0=ALU.mult
         )
-        regroup_reps(3)
         nc.vector.quantize_mx(
             out=r_codes[:].rearrange("p g n -> p (g n)").bitcast(FP8X4),
             scales=r_scales[:].rearrange("p g n -> p (g n)"),

@@ -155,10 +155,11 @@ def tile_minerva_pa_s_kernel(tc, f_norm, e_norm, ex_class_reps, out):
         for i in range(last):
             transpose_tile(i)
             copy_tile(i, vec if i == 2 else sca)
-            if i in (0, 2, 4):
+            if i in (0, 2):
                 warm()
-            if i == 6:
-                score_unit(0)
+            if i == 4:
+                score_tile(0, 0)
+                score_tile(0, 1)
             if i >= 1:
                 quantise_tile(i - 1)
         e_grouped[last] = tiles.tile([P, N_FEAT], BF16, name="e_grouped", align_bytes=64)
@@ -186,6 +187,7 @@ def tile_minerva_pa_s_kernel(tc, f_norm, e_norm, ex_class_reps, out):
                 out=r_grouped[:, g, labels, :], in_=r_rows[:, g, :, labels].rearrange("p t n -> p n t")
             )
 
+        score_tile(0, 2)
         for u in range(1, len(UNITS)):
             score_unit(u)
         idle_ps = psum_xt.tile([P, FEAT_PASSES * N_QUERY], F32, tag="xt")

@@ -160,6 +160,8 @@ def tile_minerva_pa_s_kernel(tc, f_norm, e_norm, ex_class_reps, out):
             if i == 4:
                 score_tile(0, 0)
                 score_tile(0, 1)
+            if i == 6:
+                score_tile(0, 2)
             if i >= 1:
                 quantise_tile(i - 1)
         e_grouped[last] = tiles.tile([P, N_FEAT], BF16, name="e_grouped", align_bytes=64)
@@ -187,7 +189,6 @@ def tile_minerva_pa_s_kernel(tc, f_norm, e_norm, ex_class_reps, out):
                 out=r_grouped[:, g, labels, :], in_=r_rows[:, g, :, labels].rearrange("p t n -> p n t")
             )
 
-        score_tile(0, 2)
         for u in range(1, len(UNITS)):
             score_unit(u)
         idle_ps = psum_xt.tile([P, FEAT_PASSES * N_QUERY], F32, tag="xt")

from contextlib import ExitStack

import concourse.mybir as mybir
from concourse.masks import make_identity

F32 = mybir.dt.float32
BF16 = mybir.dt.bfloat16
U32 = mybir.dt.uint32
U8 = mybir.dt.uint8
FP8X4 = mybir.dt.float8_e4m3fn_x4
ALU = mybir.AluOpType
ACT = mybir.ActivationFunctionType
AXIS = mybir.AxisListType

P = 128
PACK = 4
K_PASS = P * PACK

N_QUERY = 128
N_FEAT = 1024
N_EX = 1024
N_LABEL = 128
EPS = 1e-12

FEAT_PASSES = N_FEAT // K_PASS
EX_PASSES = N_EX // K_PASS
EX_TILES = N_EX // P
UNITS = ((0, 3), (3, 3), (6, 2))

IDLE_PASSES = 5

FLOPS = 2 * N_QUERY * N_FEAT * N_EX + 2 * N_QUERY * N_EX * N_LABEL


def tile_minerva_pa_s_kernel(tc, f_norm, e_norm, ex_class_reps, out):
    nc = tc.nc
    with ExitStack() as stack:
        stack.enter_context(tc.manual_schedule())
        keep = stack.enter_context(tc.tile_pool(name="keep", bufs=1))
        tiles = stack.enter_context(tc.tile_pool(name="tiles", bufs=EX_TILES))
        units = stack.enter_context(tc.tile_pool(name="units", bufs=len(UNITS)))
        psum_xt = stack.enter_context(tc.psum_pool(name="psum_xt", bufs=5))
        psum_s = stack.enter_context(tc.psum_pool(name="psum_s", bufs=len(UNITS)))

        e_view = e_norm.rearrange("(g h m u e) d -> g u h m e d", g=EX_PASSES, h=2, u=2, e=2)
        r_view = ex_class_reps.rearrange("(g p t) n -> p g t n", p=P, t=PACK)

        f_rows = keep.tile([P, N_FEAT], BF16)
        nc.sync.dma_start(out=f_rows[:], in_=f_norm)
        e_rows = []
        for i in range(EX_TILES):
            e_tile = tiles.tile([P, N_FEAT], BF16, name="e_tile")
            nc.sync.dma_start(out=e_tile[:], in_=e_view[i // 4, i // 2 % 2, i % 2])
            e_rows.append(e_tile)
        r_rows = keep.tile([P, EX_PASSES, PACK, N_LABEL], BF16)
        nc.sync.dma_start(out=r_rows[:], in_=r_view)

        identity = keep.tile([P, P], F32)
        make_identity(nc, identity[:])
        ones = keep.tile([P, P], F32)
        nc.vector.memset(ones[:], 1.0)
        table_warm = keep.tile([P, 1], F32)
        nc.scalar.activation(out=table_warm[:], in_=ones[:, 0:1], func=ACT.Abs)

        def transpose_words(rows, first, count):
            words = rows.bitcast(F32)
            xt = psum_xt.tile([P, count, P], F32, name="xt")
            for w in range(count):
                nc.tensor.transpose(xt[:, w, :], words[:, (first + w) * P : (first + w + 1) * P], identity[:])
            return xt

        def group_words(copy, xt, grouped):
            copy(
                out=grouped.bitcast(F32).rearrange("p (c r u) -> p c r u", r=P, u=2),
                in_=xt[:].rearrange("p (c u) r -> p c r u", u=2),
            )

        f_grouped = keep.tile([P, N_FEAT], BF16, align_bytes=64)
        f_codes = keep.tile([P, FEAT_PASSES, N_QUERY], U32, align_bytes=64)
        f_scales = keep.tile([P, FEAT_PASSES, N_QUERY], U8, align_bytes=64)

        a = keep.tile([P, N_EX], F32)
        parts = keep.tile([P, 2], F32)
        e_xt, e_grouped, e_codes, e_scales, s_ps, squares = {}, {}, {}, {}, {}, {}

        def transpose_tile(i):
            e_grouped[i] = tiles.tile([P, N_FEAT], BF16, name="e_grouped", align_bytes=64)
            e_codes[i] = tiles.tile([P, FEAT_PASSES, P], U32, name="e_codes", align_bytes=64)
            e_scales[i] = tiles.tile([P, FEAT_PASSES, P], U8, name="e_scales", align_bytes=64)
            e_xt[i] = transpose_words(e_rows[i][:], 0, 4)

        def copy_tile(i, copy):
            group_words(copy, e_xt[i], e_grouped[i][:])

        def quantise_tile(i):
            nc.vector.quantize_mx(
                out=e_codes[i][:].rearrange("p c x -> p (c x)").bitcast(FP8X4),
                scales=e_scales[i][:].rearrange("p c x -> p (c x)"),
                in_=e_grouped[i][:],
            )

        def score_tile(u, i):
            first, count = UNITS[u]
            if i == first:
                s_ps[u] = psum_s.tile([P, count, P], F32, name="s_ps")
            for c in range(FEAT_PASSES):
                nc.tensor.matmul_mx(
                    out=s_ps[u][:, i - first, :],
                    lhsT=f_codes[:, c, :].bitcast(FP8X4),
                    lhsT_scale=f_scales[:, c, :],
                    rhs=e_codes[i][:, c, :].bitcast(FP8X4),
                    rhs_scale=e_scales[i][:, c, :],
                    start=(c == 0),
                    stop=(c == FEAT_PASSES - 1),
                )

        def score_unit(u):
            first, count = UNITS[u]
            for i in range(first, first + count):
                score_tile(u, i)

        def square_unit(u):
            squares[u] = units.tile([P, UNITS[u][1], P], F32, name="squares")
            nc.scalar.activation(out=squares[u][:], in_=s_ps[u][:], func=ACT.Square)

        def unit_a(u):
            first, count = UNITS[u]
            return a[:, first * P : (first + count) * P]

        def cube_unit(u):
            nc.vector.tensor_tensor(
                out=unit_a(u),
                in0=s_ps[u][:].rearrange("p t x -> p (t x)"),
                in1=squares[u][:].rearrange("p t x -> p (t x)"),
                op=ALU.mult,
            )

        vec, sca = nc.vector.tensor_copy, nc.scalar.copy
        last = EX_TILES - 1
        half = N_FEAT // 2
        warm_ps = psum_s.tile([P, P], F32, tag="s_ps")

        def warm():
            nc.tensor.matmul(warm_ps[:], lhsT=ones[:], rhs=ones[:], start=True, stop=True)

        for k in range(3):
            warm()
        f_xt = transpose_words(f_rows[:], 0, 4)
        group_words(sca, f_xt, f_grouped[:])
        nc.vector.quantize_mx(
            out=f_codes[:].rearrange("p c q -> p (c q)").bitcast(FP8X4),
            scales=f_scales[:].rearrange("p c q -> p (c q)"),
            in_=f_grouped[:],
        )
        for i in range(last):
            transpose_tile(i)
            copy_tile(i, vec if i == 2 else sca)
            if i in (0, 2):
                warm()
            if i == 4:
                score_tile(0, 0)
                score_tile(0, 1)
            if i == 6:
                score_tile(0, 2)
            if i >= 1:
                quantise_tile(i - 1)
        e_grouped[last] = tiles.tile([P, N_FEAT], BF16, name="e_grouped", align_bytes=64)
        e_codes[last] = tiles.tile([P, FEAT_PASSES, P], U32, name="e_codes", align_bytes=64)
        e_scales[last] = tiles.tile([P, FEAT_PASSES, P], U8, name="e_scales", align_bytes=64)
        halves = [transpose_words(e_rows[last][:], 2 * c, 2) for c in range(FEAT_PASSES)]
        group_words(sca, halves[0], e_grouped[last][:, :half])
        group_words(vec, halves[1], e_grouped[last][:, half:])
        quantise_tile(last - 1)
        for c in range(FEAT_PASSES):
            nc.vector.quantize_mx(
                out=e_codes[last][:, c, :].bitcast(FP8X4),
                scales=e_scales[last][:, c, :],
                in_=e_grouped[last][:, c * half : (c + 1) * half],
            )

        r_grouped = keep.tile([P, EX_PASSES, N_LABEL, PACK], BF16, align_bytes=64)
        r_codes = keep.tile([P, EX_PASSES, N_LABEL], U32, align_bytes=64)
        r_scales = keep.tile([P, EX_PASSES, N_LABEL], U8, align_bytes=64)

        def regroup_reps(quarter):
            g, n = quarter // 2, N_LABEL // 2 * (quarter % 2)
            labels = slice(n, n + N_LABEL // 2)
            nc.vector.tensor_copy(
                out=r_grouped[:, g, labels, :], in_=r_rows[:, g, :, labels].rearrange("p t n -> p n t")
            )

        for u in range(1, len(UNITS)):
            score_unit(u)
        idle_ps = psum_xt.tile([P, FEAT_PASSES * N_QUERY], F32, tag="xt")

        def idle():
            for k in range(IDLE_PASSES):
                nc.tensor.matmul_mx(
                    out=idle_ps[:],
                    lhsT=f_codes[:, 0, :].bitcast(FP8X4),
                    lhsT_scale=f_scales[:, 0, :],
                    rhs=f_codes[:].rearrange("p c q -> p (c q)").bitcast(FP8X4),
                    rhs_scale=f_scales[:].rearrange("p c q -> p (c q)"),
                    start=True,
                    stop=True,
                )

        idle()
        for u in range(len(UNITS)):
            square_unit(u)
        for u in range(len(UNITS)):
            cube_unit(u)
        nc.tensor.matmul(idle_ps[:, :P], lhsT=a[:, last * P :], rhs=ones[:], start=True, stop=True)
        idle()

        split = UNITS[-1][0] * P
        abs_a = keep.tile([P, split], F32)
        nc.scalar.activation(out=abs_a[:], in_=a[:, :split], func=ACT.Abs, accum_out=parts[:, 0:1])
        regroup_reps(0)
        nc.vector.tensor_reduce(
            out=parts[:, 1:2], in_=a[:, split:], axis=AXIS.X, op=ALU.add, apply_absolute_value=True
        )
        regroup_reps(1)

        total = keep.tile([P, 1], F32)
        inverse = keep.tile([P, 1], F32)
        nc.vector.tensor_scalar(
            out=total[:], in0=parts[:, 1:2], scalar1=parts[:, 0:1], scalar2=EPS, op0=ALU.add, op1=ALU.max
        )
        regroup_reps(2)
        nc.vector.reciprocal(out=inverse[:], in_=total[:])
        regroup_reps(3)

        p_rows = keep.tile([P, N_EX], BF16, align_bytes=64)
        nc.vector.tensor_scalar(
            out=p_rows[:, :256], in0=a[:, :256], scalar1=inverse[:, 0:1], scalar2=None, op0=ALU.mult
        )
        nc.scalar.activation(out=p_rows[:, 256:512], in_=a[:, 256:512], func=ACT.Copy, scale=inverse[:, 0:1])
        nc.vector.tensor_scalar(
            out=p_rows[:, 512:], in0=a[:, 512:], scalar1=inverse[:, 0:1], scalar2=None, op0=ALU.mult
        )
        nc.vector.quantize_mx(
            out=r_codes[:].rearrange("p g n -> p (g n)").bitcast(FP8X4),
            scales=r_scales[:].rearrange("p g n -> p (g n)"),
            in_=r_grouped[:].rearrange("p g n t -> p (g n t)"),
        )
        p_grouped = keep.tile([P, EX_PASSES, N_QUERY * PACK], BF16, align_bytes=64)
        p_codes = keep.tile([P, EX_PASSES, N_QUERY], U32, align_bytes=64)
        p_scales = keep.tile([P, EX_PASSES, N_QUERY], U8, align_bytes=64)
        p_xt = [transpose_words(p_rows[:], 2 * g, 2) for g in range(EX_PASSES)]
        for g in range(EX_PASSES):
            group_words(sca, p_xt[g], p_grouped[:, g, :])
        for g in range(EX_PASSES):
            nc.vector.quantize_mx(
                out=p_codes[:, g, :].bitcast(FP8X4),
                scales=p_scales[:, g, :],
                in_=p_grouped[:, g, :],
            )

        echo_ps = psum_s.tile([P, N_LABEL], F32, tag="s_ps")
        for g in range(EX_PASSES):
            nc.tensor.matmul_mx(
                out=echo_ps[:],
                lhsT=p_codes[:, g, :].bitcast(FP8X4),
                lhsT_scale=p_scales[:, g, :],
                rhs=r_codes[:, g, :].bitcast(FP8X4),
                rhs_scale=r_scales[:, g, :],
                start=(g == 0),
                stop=(g == EX_PASSES - 1),
            )
        echo = keep.tile([P, N_LABEL], F32)
        nc.scalar.copy(out=echo[:], in_=echo_ps[:])
        nc.sync.dma_start(out=out, in_=echo[:])
